import numpy as np
import ml_dtypes


def mxq(x, axis, fmt="e4m3"):
    dtype, down = {"e4m3": (ml_dtypes.float8_e4m3fn, 7), "e5m2": (ml_dtypes.float8_e5m2, 14)}[fmt]
    v = np.moveaxis(np.asarray(x, np.float32).astype(ml_dtypes.bfloat16).astype(np.float64), axis, -1)
    blocks = v.reshape(v.shape[:-1] + (-1, 32))
    amax = np.abs(blocks).max(-1, keepdims=True)
    byte = np.maximum(np.where(amax > 0, np.frexp(amax)[1] - 1 + 127, 0) - down, 1)
    scale = np.exp2(byte - 127.0)
    codes = (blocks / scale).astype(np.float32).astype(dtype).astype(np.float64)
    return np.moveaxis((codes * scale).reshape(v.shape), -1, axis)


WIDE = False


def mx_kscale(k):
    if not WIDE:
        return np.ones(k)
    levels = np.array([10, -10, 5, -5, 0])
    a = np.random.permutation(np.resize(levels, k // 512 * 4)).reshape(k // 512, 4)
    idx = np.arange(k)
    return np.exp2(a[idx // 512, idx % 128 // 32])


BF16 = ml_dtypes.bfloat16


def bf(x):
    return np.asarray(x, np.float32).astype(BF16)


def f64(x):
    return np.asarray(x).astype(np.float64)


B, P0, P1, P2, K0, K1, K2 = 4096, 512, 512, 512, 128, 128, 128
PT = P0 + P1 + P2
KT = K0 + K1 + K2
CLIP0 = 1.0


def clip_rows(mat, clip):
    norms = np.sqrt(np.sum(mat * mat, axis=1, keepdims=True))
    scale = np.minimum(clip / norms, 1.0)
    return mat * scale


def setup_inputs():
    s0, s1, s2 = mx_kscale(P0), mx_kscale(P1), mx_kscale(P2)
    r = np.exp2(np.random.uniform(-2.0, 2.0, (B, 1))) / (KT * PT) ** 0.25
    return {"target_grad": bf(np.random.standard_normal((B, PT)) * r * np.concatenate([s0, s1, s2])),
            "bases0": bf(np.random.standard_normal((P0, K0)) / np.sqrt(P0) / s0[:, None]),
            "bases1": bf(np.random.standard_normal((P1, K1)) / np.sqrt(P1) / s1[:, None]),
            "bases2": bf(np.random.standard_normal((P2, K2)) / np.sqrt(P2) / s2[:, None])}


def reference(target_grad, bases0, bases1, bases2):
    g = f64(target_grad)
    embeddings = []
    offset = 0
    for b in (f64(bases0), f64(bases1), f64(bases2)):
        num_p = b.shape[0]
        embeddings.append(mxq(g[:, offset:offset + num_p], 1, "e4m3") @ mxq(b, 0, "e4m3"))
        offset += num_p
    embedding = np.concatenate(embeddings, axis=1)
    avg_clipped_embedding = np.sum(clip_rows(embedding, CLIP0), axis=0) / B
    return embedding, avg_clipped_embedding

@@ -1,0 +1,195 @@
+from contextlib import ExitStack
+
+import concourse.mybir as mybir
+from concourse.masks import make_identity
+
+F32 = mybir.dt.float32
+BF16 = mybir.dt.bfloat16
+U32 = mybir.dt.uint32
+U8 = mybir.dt.uint8
+FP8X4 = mybir.dt.float8_e4m3fn_x4
+ACT = mybir.ActivationFunctionType
+ALU = mybir.AluOpType
+AXIS = mybir.AxisListType
+
+P = 128
+PACK = 4
+HALVES = 2
+BATCH = 4096
+GROUPS = 3
+K_GROUP = P * PACK
+WORDS_GROUP = K_GROUP // 2
+EMB = 128
+EMB_ALL = GROUPS * EMB
+TILES = 2
+UNITS = BATCH // (TILES * P)
+ROW_TILES = UNITS * TILES
+CLIP = 1.0
+
+FLOPS = 2 * BATCH * GROUPS * K_GROUP * EMB
+
+
+def tile_gep_pa_t_kernel(tc, target_grad, bases0, bases1, bases2, out_0, out_1):
+    nc = tc.nc
+    bases = [bases0, bases1, bases2]
+
+    grad_units = target_grad.rearrange("(u p t) k -> u p (t k)", p=P, t=TILES)
+    emb_units = out_0.rearrange("(u p t) j -> u p (t j)", p=P, t=TILES)
+
+    with ExitStack() as ctx:
+        ctx.enter_context(tc.manual_schedule())
+        const = ctx.enter_context(tc.tile_pool(name="const", bufs=1))
+        grads = ctx.enter_context(tc.tile_pool(name="grads", bufs=UNITS))
+        stage = ctx.enter_context(tc.tile_pool(name="stage", bufs=3))
+        embs = ctx.enter_context(tc.tile_pool(name="embs", bufs=6))
+        flipped_psum = ctx.enter_context(tc.psum_pool(name="flipped_psum", bufs=4))
+        emb_psum = ctx.enter_context(tc.psum_pool(name="emb_psum", bufs=3))
+        mean_psum = ctx.enter_context(tc.psum_pool(name="mean_psum", bufs=1))
+
+        grad_sb = []
+        for u in range(UNITS):
+            grad = grads.tile([P, TILES, GROUPS * K_GROUP], BF16)
+            nc.sync.dma_start(out=grad[:].rearrange("p t k -> p (t k)"), in_=grad_units[u])
+            grad_sb.append(grad)
+
+        base_rows = const.tile([P, GROUPS, PACK, EMB], BF16)
+        for g in range(GROUPS):
+            nc.scalar.dma_start(
+                out=base_rows[:, g].rearrange("p (h e) c -> p h (e c)", h=HALVES),
+                in_=bases[g].rearrange("(h p e) c -> p h (e c)", h=HALVES, p=P),
+            )
+
+        identity = const.tile([P, P], F32)
+        make_identity(nc, identity[:])
+        ones = const.tile([P, 1], F32)
+        nc.vector.memset(ones[:], 1.0)
+        warm = const.tile([P, 1], F32)
+        nc.scalar.activation(out=warm[:], in_=ones[:], func=ACT.Abs_reciprocal_sqrt)
+        column_sums = const.tile([P, P], F32)
+        nc.vector.memset(column_sums[:], 0.0)
+
+        square_sums = const.tile([P, ROW_TILES], F32)
+        floored = const.tile([P, ROW_TILES], F32)
+        factor = const.tile([P, ROW_TILES], F32)
+        mean_parts = mean_psum.tile([P, GROUPS, ROW_TILES], F32)
+
+        base_grouped = const.tile([P, GROUPS, EMB, PACK], BF16, align_bytes=64)
+        nc.vector.tensor_copy(
+            out=base_grouped[:], in_=base_rows[:].rearrange("p g t c -> p g c t")
+        )
+        base_codes = const.tile([P, GROUPS, EMB], U32, align_bytes=64)
+        base_scales = const.tile([P, GROUPS, EMB], U8, align_bytes=64)
+        for g in range(GROUPS):
+            nc.vector.quantize_mx(
+                out=base_codes[:, g, :].bitcast(FP8X4),
+                scales=base_scales[:, g, :],
+                in_=base_grouped[:, g].rearrange("p c t -> p (c t)"),
+            )
+
+        grouped_sb = {}
+        codes_sb = {}
+        scales_sb = {}
+        emb_sb = {}
+
+        def flip_and_regroup(u):
+            words = grad_sb[u][:].bitcast(F32)
+            grouped = stage.tile([P, GROUPS, TILES * P * PACK], BF16, align_bytes=64)
+            grouped_sb[u] = grouped
+            for g in range(GROUPS):
+                flipped = flipped_psum.tile([P, TILES, HALVES, P], F32)
+                for t in range(TILES):
+                    for h in range(HALVES):
+                        first = WORDS_GROUP * g + P * h
+                        nc.tensor.transpose(
+                            flipped[:, t, h, :], words[:, t, first : first + P], identity[:]
+                        )
+                copy = nc.scalar.copy if g == GROUPS - 1 else nc.vector.tensor_copy
+                copy(
+                    out=grouped[:, g, :]
+                    .bitcast(F32)
+                    .rearrange("p (t b h) -> p t b h", t=TILES, h=HALVES),
+                    in_=flipped[:].rearrange("p t h b -> p t b h"),
+                )
+
+        def quantise(u):
+            codes = stage.tile([P, GROUPS, TILES * P], U32, align_bytes=64)
+            scales = stage.tile([P, GROUPS, TILES * P], U8, align_bytes=64)
+            codes_sb[u] = codes
+            scales_sb[u] = scales
+            for g in range(GROUPS):
+                nc.vector.quantize_mx(
+                    out=codes[:, g, :].bitcast(FP8X4),
+                    scales=scales[:, g, :],
+                    in_=grouped_sb[u][:, g, :],
+                )
+
+        def project(u):
+            emb = embs.tile([P, TILES, EMB_ALL], F32)
+            emb_sb[u] = emb
+            for t in range(TILES):
+                rows = slice(t * P, (t + 1) * P)
+                acc = emb_psum.tile([P, EMB_ALL], F32)
+                for g in range(GROUPS):
+                    nc.tensor.matmul_mx(
+                        out=acc[:, g * EMB : (g + 1) * EMB],
+                        lhsT=codes_sb[u][:, g, rows].bitcast(FP8X4),
+                        lhsT_scale=scales_sb[u][:, g, rows],
+                        rhs=base_codes[:, g, :].bitcast(FP8X4),
+                        rhs_scale=base_scales[:, g, :],
+                        start=True,
+                        stop=True,
+                    )
+                nc.scalar.copy(out=emb[:, t, :], in_=acc[:])
+                squares = stage.tile([P, EMB_ALL], F32)
+                n = u * TILES + t
+                nc.scalar.activation(
+                    out=squares[:],
+                    in_=emb[:, t, :],
+                    func=ACT.Square,
+                    accum_out=square_sums[:, n : n + 1],
+                )
+            nc.sync.dma_start(out=emb_units[u], in_=emb[:].rearrange("p t j -> p (t j)"))
+
+        def clip_factor(u):
+            cols = slice(u * TILES, (u + 1) * TILES)
+            nc.vector.tensor_scalar_max(floored[:, cols], square_sums[:, cols], CLIP * CLIP)
+            nc.scalar.activation(
+                out=factor[:, cols], in_=floored[:, cols], func=ACT.Abs_reciprocal_sqrt
+            )
+
+        def mean_part(u):
+            for t in range(TILES):
+                n = u * TILES + t
+                for g in range(GROUPS):
+                    nc.tensor.matmul(
+                        out=mean_parts[:, g, n : n + 1],
+                        lhsT=emb_sb[u][:, t, g * EMB : (g + 1) * EMB],
+                        rhs=factor[:, n : n + 1],
+                        start=True,
+                        stop=True,
+                    )
+
+        for step in range(UNITS + 3):
+            if 0 <= step - 1 < UNITS:
+                quantise(step - 1)
+            if step < UNITS:
+                flip_and_regroup(step)
+            if 0 <= step - 1 < UNITS:
+                project(step - 1)
+            if 0 <= step - 2 < UNITS:
+                clip_factor(step - 2)
+            if 0 <= step - 3 < UNITS:
+                mean_part(step - 3)
+
+        nc.vector.tensor_reduce(
+            out=column_sums[:, 0:GROUPS], in_=mean_parts[:], axis=AXIS.X, op=ALU.add
+        )
+        sums_flipped = flipped_psum.tile([P, TILES, HALVES, P], F32, tag="flipped")
+        nc.tensor.transpose(sums_flipped[:, 0, 0, :], column_sums[:], identity[:])
+        avg = const.tile([P, EMB], F32)
+        nc.scalar.activation(
+            out=avg[:], in_=sums_flipped[:, 0, 0, :], func=ACT.Copy, scale=CLIP / BATCH
+        )
+        nc.sync.dma_start(
+            out=out_1.rearrange("(g j) -> g j", g=GROUPS), in_=avg[0:GROUPS, :]
+        )

@@ -10,7 +10,6 @@ U8 = mybir.dt.uint8
 FP8X4 = mybir.dt.float8_e4m3fn_x4
 ACT = mybir.ActivationFunctionType
 ALU = mybir.AluOpType
-AXIS = mybir.AxisListType
 
 P = 128
 PACK = 4
@@ -23,7 +22,6 @@ EMB = 128
 EMB_ALL = GROUPS * EMB
 TILES = 2
 UNITS = BATCH // (TILES * P)
-ROW_TILES = UNITS * TILES
 CLIP = 1.0
 
 FLOPS = 2 * BATCH * GROUPS * K_GROUP * EMB
@@ -41,10 +39,10 @@ def tile_gep_pa_t_kernel(tc, target_grad, bases0, bases1, bases2, out_0, out_1):
         const = ctx.enter_context(tc.tile_pool(name="const", bufs=1))
         grads = ctx.enter_context(tc.tile_pool(name="grads", bufs=UNITS))
         stage = ctx.enter_context(tc.tile_pool(name="stage", bufs=3))
-        embs = ctx.enter_context(tc.tile_pool(name="embs", bufs=6))
-        flipped_psum = ctx.enter_context(tc.psum_pool(name="flipped_psum", bufs=4))
+        embs = ctx.enter_context(tc.tile_pool(name="embs", bufs=UNITS))
+        small = ctx.enter_context(tc.tile_pool(name="small", bufs=6))
+        flipped_psum = ctx.enter_context(tc.psum_pool(name="flipped_psum", bufs=5))
         emb_psum = ctx.enter_context(tc.psum_pool(name="emb_psum", bufs=3))
-        mean_psum = ctx.enter_context(tc.psum_pool(name="mean_psum", bufs=1))
 
         grad_sb = []
         for u in range(UNITS):
@@ -65,13 +63,10 @@ def tile_gep_pa_t_kernel(tc, target_grad, bases0, bases1, bases2, out_0, out_1):
         nc.vector.memset(ones[:], 1.0)
         warm = const.tile([P, 1], F32)
         nc.scalar.activation(out=warm[:], in_=ones[:], func=ACT.Abs_reciprocal_sqrt)
-        column_sums = const.tile([P, P], F32)
-        nc.vector.memset(column_sums[:], 0.0)
-
-        square_sums = const.tile([P, ROW_TILES], F32)
-        floored = const.tile([P, ROW_TILES], F32)
-        factor = const.tile([P, ROW_TILES], F32)
-        mean_parts = mean_psum.tile([P, GROUPS, ROW_TILES], F32)
+        weighted = const.tile([P, TILES, EMB_ALL], F32)
+        nc.vector.memset(weighted[:], 0.0)
+        averager = const.tile([P, P], F32)
+        nc.vector.memset(averager[:], CLIP / BATCH)
 
         base_grouped = const.tile([P, GROUPS, EMB, PACK], BF16, align_bytes=64)
         nc.vector.tensor_copy(
@@ -90,6 +85,8 @@ def tile_gep_pa_t_kernel(tc, target_grad, bases0, bases1, bases2, out_0, out_1):
         codes_sb = {}
         scales_sb = {}
         emb_sb = {}
+        square_sum_sb = {}
+        factor_sb = {}
 
         def flip_and_regroup(u):
             words = grad_sb[u][:].bitcast(F32)
@@ -103,7 +100,7 @@ def tile_gep_pa_t_kernel(tc, target_grad, bases0, bases1, bases2, out_0, out_1):
                         nc.tensor.transpose(
                             flipped[:, t, h, :], words[:, t, first : first + P], identity[:]
                         )
-                copy = nc.scalar.copy if g == GROUPS - 1 else nc.vector.tensor_copy
+                copy = nc.vector.tensor_copy if (u * GROUPS + g) % 2 == 0 else nc.scalar.copy
                 copy(
                     out=grouped[:, g, :]
                     .bitcast(F32)
@@ -126,6 +123,8 @@ def tile_gep_pa_t_kernel(tc, target_grad, bases0, bases1, bases2, out_0, out_1):
         def project(u):
             emb = embs.tile([P, TILES, EMB_ALL], F32)
             emb_sb[u] = emb
+            square_sum = small.tile([P, TILES], F32)
+            square_sum_sb[u] = square_sum
             for t in range(TILES):
                 rows = slice(t * P, (t + 1) * P)
                 acc = emb_psum.tile([P, EMB_ALL], F32)
@@ -141,33 +140,31 @@ def tile_gep_pa_t_kernel(tc, target_grad, bases0, bases1, bases2, out_0, out_1):
                     )
                 nc.scalar.copy(out=emb[:, t, :], in_=acc[:])
                 squares = stage.tile([P, EMB_ALL], F32)
-                n = u * TILES + t
                 nc.scalar.activation(
                     out=squares[:],
                     in_=emb[:, t, :],
                     func=ACT.Square,
-                    accum_out=square_sums[:, n : n + 1],
+                    accum_out=square_sum[:, t : t + 1],
                 )
             nc.sync.dma_start(out=emb_units[u], in_=emb[:].rearrange("p t j -> p (t j)"))
 
         def clip_factor(u):
-            cols = slice(u * TILES, (u + 1) * TILES)
-            nc.vector.tensor_scalar_max(floored[:, cols], square_sums[:, cols], CLIP * CLIP)
-            nc.scalar.activation(
-                out=factor[:, cols], in_=floored[:, cols], func=ACT.Abs_reciprocal_sqrt
-            )
+            floored = small.tile([P, TILES], F32)
+            nc.vector.tensor_scalar_max(floored[:], square_sum_sb[u][:], CLIP * CLIP)
+            factor = small.tile([P, TILES], F32)
+            factor_sb[u] = factor
+            nc.scalar.activation(out=factor[:], in_=floored[:], func=ACT.Abs_reciprocal_sqrt)
 
-        def mean_part(u):
+        def weigh(u):
             for t in range(TILES):
-                n = u * TILES + t
-                for g in range(GROUPS):
-                    nc.tensor.matmul(
-                        out=mean_parts[:, g, n : n + 1],
-                        lhsT=emb_sb[u][:, t, g * EMB : (g + 1) * EMB],
-                        rhs=factor[:, n : n + 1],
-                        start=True,
-                        stop=True,
-                    )
+                nc.vector.scalar_tensor_tensor(
+                    out=weighted[:, t, :],
+                    in0=emb_sb[u][:, t, :],
+                    scalar=factor_sb[u][:, t : t + 1],
+                    in1=weighted[:, t, :],
+                    op0=ALU.mult,
+                    op1=ALU.add,
+                )
 
         for step in range(UNITS + 3):
             if 0 <= step - 1 < UNITS:
@@ -179,17 +176,12 @@ def tile_gep_pa_t_kernel(tc, target_grad, bases0, bases1, bases2, out_0, out_1):
             if 0 <= step - 2 < UNITS:
                 clip_factor(step - 2)
             if 0 <= step - 3 < UNITS:
-                mean_part(step - 3)
+                weigh(step - 3)
 
-        nc.vector.tensor_reduce(
-            out=column_sums[:, 0:GROUPS], in_=mean_parts[:], axis=AXIS.X, op=ALU.add
-        )
-        sums_flipped = flipped_psum.tile([P, TILES, HALVES, P], F32, tag="flipped")
-        nc.tensor.transpose(sums_flipped[:, 0, 0, :], column_sums[:], identity[:])
-        avg = const.tile([P, EMB], F32)
-        nc.scalar.activation(
-            out=avg[:], in_=sums_flipped[:, 0, 0, :], func=ACT.Copy, scale=CLIP / BATCH
-        )
-        nc.sync.dma_start(
-            out=out_1.rearrange("(g j) -> g j", g=GROUPS), in_=avg[0:GROUPS, :]
-        )
+        total = const.tile([P, EMB_ALL], F32)
+        nc.vector.tensor_add(out=total[:], in0=weighted[:, 0, :], in1=weighted[:, 1, :])
+        mean_all = emb_psum.tile([P, EMB_ALL], F32, tag="acc")
+        nc.tensor.matmul(out=mean_all[:], lhsT=averager[:], rhs=total[:], start=True, stop=True)
+        avg = const.tile([P, EMB_ALL], F32)
+        nc.scalar.copy(out=avg[:], in_=mean_all[:])
+        nc.sync.dma_start(out=out_1.rearrange("(o j) -> o j", o=1), in_=avg[0:1, :])

@@ -10,6 +10,7 @@ U8 = mybir.dt.uint8
 FP8X4 = mybir.dt.float8_e4m3fn_x4
 ACT = mybir.ActivationFunctionType
 ALU = mybir.AluOpType
+AXIS = mybir.AxisListType
 
 P = 128
 PACK = 4
@@ -41,8 +42,9 @@ def tile_gep_pa_t_kernel(tc, target_grad, bases0, bases1, bases2, out_0, out_1):
         stage = ctx.enter_context(tc.tile_pool(name="stage", bufs=3))
         embs = ctx.enter_context(tc.tile_pool(name="embs", bufs=UNITS))
         small = ctx.enter_context(tc.tile_pool(name="small", bufs=6))
-        flipped_psum = ctx.enter_context(tc.psum_pool(name="flipped_psum", bufs=5))
+        flipped_psum = ctx.enter_context(tc.psum_pool(name="flipped_psum", bufs=4))
         emb_psum = ctx.enter_context(tc.psum_pool(name="emb_psum", bufs=3))
+        mean_psum = ctx.enter_context(tc.psum_pool(name="mean_psum", bufs=1))
 
         grad_sb = []
         for u in range(UNITS):
@@ -63,10 +65,9 @@ def tile_gep_pa_t_kernel(tc, target_grad, bases0, bases1, bases2, out_0, out_1):
         nc.vector.memset(ones[:], 1.0)
         warm = const.tile([P, 1], F32)
         nc.scalar.activation(out=warm[:], in_=ones[:], func=ACT.Abs_reciprocal_sqrt)
-        weighted = const.tile([P, TILES, EMB_ALL], F32)
-        nc.vector.memset(weighted[:], 0.0)
-        averager = const.tile([P, P], F32)
-        nc.vector.memset(averager[:], CLIP / BATCH)
+        column_sums = const.tile([P, P], F32)
+        nc.vector.memset(column_sums[:], 0.0)
+        weighted = mean_psum.tile([P, GROUPS, P], F32)
 
         base_grouped = const.tile([P, GROUPS, EMB, PACK], BF16, align_bytes=64)
         nc.vector.tensor_copy(
@@ -87,6 +88,7 @@ def tile_gep_pa_t_kernel(tc, target_grad, bases0, bases1, bases2, out_0, out_1):
         emb_sb = {}
         square_sum_sb = {}
         factor_sb = {}
+        scaled_sb = {}
 
         def flip_and_regroup(u):
             words = grad_sb[u][:].bitcast(F32)
@@ -100,7 +102,7 @@ def tile_gep_pa_t_kernel(tc, target_grad, bases0, bases1, bases2, out_0, out_1):
                         nc.tensor.transpose(
                             flipped[:, t, h, :], words[:, t, first : first + P], identity[:]
                         )
-                copy = nc.vector.tensor_copy if (u * GROUPS + g) % 2 == 0 else nc.scalar.copy
+                copy = nc.scalar.copy if g == GROUPS - 1 else nc.vector.tensor_copy
                 copy(
                     out=grouped[:, g, :]
                     .bitcast(F32)
@@ -156,21 +158,32 @@ def tile_gep_pa_t_kernel(tc, target_grad, bases0, bases1, bases2, out_0, out_1):
             nc.scalar.activation(out=factor[:], in_=floored[:], func=ACT.Abs_reciprocal_sqrt)
 
         def weigh(u):
+            scaled = stage.tile([P, TILES, EMB_ALL], F32)
+            scaled_sb[u] = scaled
             for t in range(TILES):
-                nc.vector.scalar_tensor_tensor(
-                    out=weighted[:, t, :],
-                    in0=emb_sb[u][:, t, :],
-                    scalar=factor_sb[u][:, t : t + 1],
-                    in1=weighted[:, t, :],
-                    op0=ALU.mult,
-                    op1=ALU.add,
+                nc.vector.tensor_scalar_mul(
+                    scaled[:, t, :], emb_sb[u][:, t, :], factor_sb[u][:, t : t + 1]
                 )
 
-        for step in range(UNITS + 3):
+        def add_up(u):
+            for t in range(TILES):
+                for g in range(GROUPS):
+                    nc.tensor.matmul(
+                        out=weighted[:, g, :],
+                        lhsT=scaled_sb[u][:, t, g * EMB : (g + 1) * EMB],
+                        rhs=identity[:],
+                        is_transpose=True,
+                        start=(u == 0 and t == 0 and g == 0),
+                        stop=(u == UNITS - 1 and t == TILES - 1 and g == GROUPS - 1),
+                    )
+
+        for step in range(UNITS + 4):
             if 0 <= step - 1 < UNITS:
                 quantise(step - 1)
             if step < UNITS:
                 flip_and_regroup(step)
+            if 0 <= step - 4 < UNITS:
+                add_up(step - 4)
             if 0 <= step - 1 < UNITS:
                 project(step - 1)
             if 0 <= step - 2 < UNITS:
@@ -178,10 +191,15 @@ def tile_gep_pa_t_kernel(tc, target_grad, bases0, bases1, bases2, out_0, out_1):
             if 0 <= step - 3 < UNITS:
                 weigh(step - 3)
 
-        total = const.tile([P, EMB_ALL], F32)
-        nc.vector.tensor_add(out=total[:], in0=weighted[:, 0, :], in1=weighted[:, 1, :])
-        mean_all = emb_psum.tile([P, EMB_ALL], F32, tag="acc")
-        nc.tensor.matmul(out=mean_all[:], lhsT=averager[:], rhs=total[:], start=True, stop=True)
-        avg = const.tile([P, EMB_ALL], F32)
-        nc.scalar.copy(out=avg[:], in_=mean_all[:])
-        nc.sync.dma_start(out=out_1.rearrange("(o j) -> o j", o=1), in_=avg[0:1, :])
+        nc.vector.tensor_reduce(
+            out=column_sums[:, 0:GROUPS], in_=weighted[:], axis=AXIS.X, op=ALU.add
+        )
+        sums_flipped = flipped_psum.tile([P, TILES, HALVES, P], F32, tag="flipped")
+        nc.tensor.transpose(sums_flipped[:, 0, 0, :], column_sums[:], identity[:])
+        avg = const.tile([P, EMB], F32)
+        nc.scalar.activation(
+            out=avg[:], in_=sums_flipped[:, 0, 0, :], func=ACT.Copy, scale=CLIP / BATCH
+        )
+        nc.sync.dma_start(
+            out=out_1.rearrange("(g j) -> g j", g=GROUPS), in_=avg[0:GROUPS, :]
+        )

@@ -161,8 +161,13 @@ def tile_gep_pa_t_kernel(tc, target_grad, bases0, bases1, bases2, out_0, out_1):
             scaled = stage.tile([P, TILES, EMB_ALL], F32)
             scaled_sb[u] = scaled
             for t in range(TILES):
-                nc.vector.tensor_scalar_mul(
-                    scaled[:, t, :], emb_sb[u][:, t, :], factor_sb[u][:, t : t + 1]
+                nc.gpsimd.tensor_scalar(
+                    out=scaled[:, t, :],
+                    in0=emb_sb[u][:, t, :],
+                    scalar1=factor_sb[u][:, t : t + 1],
+                    scalar2=0.0,
+                    op0=ALU.mult,
+                    op1=ALU.add,
                 )
 
         def add_up(u):

@@ -18,7 +18,6 @@ HALVES = 2
 BATCH = 4096
 GROUPS = 3
 K_GROUP = P * PACK
-WORDS_GROUP = K_GROUP // 2
 EMB = 128
 EMB_ALL = GROUPS * EMB
 TILES = 2
@@ -32,7 +31,7 @@ def tile_gep_pa_t_kernel(tc, target_grad, bases0, bases1, bases2, out_0, out_1):
     nc = tc.nc
     bases = [bases0, bases1, bases2]
 
-    grad_units = target_grad.rearrange("(u p t) k -> u p (t k)", p=P, t=TILES)
+    grad_pieces = target_grad.rearrange("(u p t) (g k) -> u g p t k", p=P, t=TILES, g=GROUPS)
     emb_units = out_0.rearrange("(u p t) j -> u p (t j)", p=P, t=TILES)
 
     with ExitStack() as ctx:
@@ -48,8 +47,9 @@ def tile_gep_pa_t_kernel(tc, target_grad, bases0, bases1, bases2, out_0, out_1):
 
         grad_sb = []
         for u in range(UNITS):
-            grad = grads.tile([P, TILES, GROUPS * K_GROUP], BF16)
-            nc.sync.dma_start(out=grad[:].rearrange("p t k -> p (t k)"), in_=grad_units[u])
+            grad = grads.tile([P, GROUPS, TILES, K_GROUP], BF16)
+            for g in range(GROUPS):
+                nc.sync.dma_start(out=grad[:, g], in_=grad_pieces[u, g])
             grad_sb.append(grad)
 
         base_rows = const.tile([P, GROUPS, PACK, EMB], BF16)
@@ -61,10 +61,8 @@ def tile_gep_pa_t_kernel(tc, target_grad, bases0, bases1, bases2, out_0, out_1):
 
         identity = const.tile([P, P], F32)
         make_identity(nc, identity[:])
-        ones = const.tile([P, 1], F32)
-        nc.vector.memset(ones[:], 1.0)
-        warm = const.tile([P, 1], F32)
-        nc.scalar.activation(out=warm[:], in_=ones[:], func=ACT.Abs_reciprocal_sqrt)
+        minus_half = const.tile([P, TILES], F32)
+        nc.gpsimd.memset(minus_half[:], -0.5)
         column_sums = const.tile([P, P], F32)
         nc.vector.memset(column_sums[:], 0.0)
         weighted = mean_psum.tile([P, GROUPS, P], F32)
@@ -91,18 +89,17 @@ def tile_gep_pa_t_kernel(tc, target_grad, bases0, bases1, bases2, out_0, out_1):
         scaled_sb = {}
 
         def flip_and_regroup(u):
-            words = grad_sb[u][:].bitcast(F32)
             grouped = stage.tile([P, GROUPS, TILES * P * PACK], BF16, align_bytes=64)
             grouped_sb[u] = grouped
             for g in range(GROUPS):
                 flipped = flipped_psum.tile([P, TILES, HALVES, P], F32)
                 for t in range(TILES):
+                    words = grad_sb[u][:, g, t, :].bitcast(F32)
                     for h in range(HALVES):
-                        first = WORDS_GROUP * g + P * h
                         nc.tensor.transpose(
-                            flipped[:, t, h, :], words[:, t, first : first + P], identity[:]
+                            flipped[:, t, h, :], words[:, h * P : (h + 1) * P], identity[:]
                         )
-                copy = nc.scalar.copy if g == GROUPS - 1 else nc.vector.tensor_copy
+                copy = nc.scalar.copy if g == 1 else nc.vector.tensor_copy
                 copy(
                     out=grouped[:, g, :]
                     .bitcast(F32)
@@ -127,9 +124,11 @@ def tile_gep_pa_t_kernel(tc, target_grad, bases0, bases1, bases2, out_0, out_1):
             emb_sb[u] = emb
             square_sum = small.tile([P, TILES], F32)
             square_sum_sb[u] = square_sum
+            accs = []
             for t in range(TILES):
                 rows = slice(t * P, (t + 1) * P)
                 acc = emb_psum.tile([P, EMB_ALL], F32)
+                accs.append(acc)
                 for g in range(GROUPS):
                     nc.tensor.matmul_mx(
                         out=acc[:, g * EMB : (g + 1) * EMB],
@@ -140,34 +139,31 @@ def tile_gep_pa_t_kernel(tc, target_grad, bases0, bases1, bases2, out_0, out_1):
                         start=True,
                         stop=True,
                     )
-                nc.scalar.copy(out=emb[:, t, :], in_=acc[:])
+            for t in range(TILES):
                 squares = stage.tile([P, EMB_ALL], F32)
                 nc.scalar.activation(
                     out=squares[:],
-                    in_=emb[:, t, :],
+                    in_=accs[t][:],
                     func=ACT.Square,
                     accum_out=square_sum[:, t : t + 1],
                 )
+            for t in range(TILES):
+                nc.scalar.copy(out=emb[:, t, :], in_=accs[t][:])
             nc.sync.dma_start(out=emb_units[u], in_=emb[:].rearrange("p t j -> p (t j)"))
 
         def clip_factor(u):
             floored = small.tile([P, TILES], F32)
-            nc.vector.tensor_scalar_max(floored[:], square_sum_sb[u][:], CLIP * CLIP)
+            nc.gpsimd.tensor_scalar_max(floored[:], square_sum_sb[u][:], CLIP * CLIP)
             factor = small.tile([P, TILES], F32)
             factor_sb[u] = factor
-            nc.scalar.activation(out=factor[:], in_=floored[:], func=ACT.Abs_reciprocal_sqrt)
+            nc.gpsimd.tensor_tensor(out=factor[:], in0=floored[:], in1=minus_half[:], op=ALU.pow)
 
         def weigh(u):
             scaled = stage.tile([P, TILES, EMB_ALL], F32)
             scaled_sb[u] = scaled
             for t in range(TILES):
-                nc.gpsimd.tensor_scalar(
-                    out=scaled[:, t, :],
-                    in0=emb_sb[u][:, t, :],
-                    scalar1=factor_sb[u][:, t : t + 1],
-                    scalar2=0.0,
-                    op0=ALU.mult,
-                    op1=ALU.add,
+                nc.vector.tensor_scalar_mul(
+                    scaled[:, t, :], emb_sb[u][:, t, :], factor_sb[u][:, t : t + 1]
                 )
 
         def add_up(u):
@@ -182,19 +178,18 @@ def tile_gep_pa_t_kernel(tc, target_grad, bases0, bases1, bases2, out_0, out_1):
                         stop=(u == UNITS - 1 and t == TILES - 1 and g == GROUPS - 1),
                     )
 
-        for step in range(UNITS + 4):
+        for step in range(UNITS + 3):
             if 0 <= step - 1 < UNITS:
                 quantise(step - 1)
             if step < UNITS:
                 flip_and_regroup(step)
-            if 0 <= step - 4 < UNITS:
-                add_up(step - 4)
+            if 0 <= step - 3 < UNITS:
+                add_up(step - 3)
             if 0 <= step - 1 < UNITS:
                 project(step - 1)
+                clip_factor(step - 1)
             if 0 <= step - 2 < UNITS:
-                clip_factor(step - 2)
-            if 0 <= step - 3 < UNITS:
-                weigh(step - 3)
+                weigh(step - 2)
 
         nc.vector.tensor_reduce(
             out=column_sums[:, 0:GROUPS], in_=weighted[:], axis=AXIS.X, op=ALU.add

@@ -23,6 +23,8 @@ EMB_ALL = GROUPS * EMB
 TILES = 2
 UNITS = BATCH // (TILES * P)
 CLIP = 1.0
+SCALAR_BANKS = 3
+OF_BANKS = 8
 
 FLOPS = 2 * BATCH * GROUPS * K_GROUP * EMB
 
@@ -99,7 +101,9 @@ def tile_gep_pa_t_kernel(tc, target_grad, bases0, bases1, bases2, out_0, out_1):
                         nc.tensor.transpose(
                             flipped[:, t, h, :], words[:, h * P : (h + 1) * P], identity[:]
                         )
-                copy = nc.scalar.copy if g == 1 else nc.vector.tensor_copy
+                bank = u * GROUPS + g
+                to_scalar = (bank * SCALAR_BANKS) % OF_BANKS < SCALAR_BANKS
+                copy = nc.scalar.copy if to_scalar else nc.vector.tensor_copy
                 copy(
                     out=grouped[:, g, :]
                     .bitcast(F32)
@@ -112,11 +116,11 @@ def tile_gep_pa_t_kernel(tc, target_grad, bases0, bases1, bases2, out_0, out_1):
             scales = stage.tile([P, GROUPS, TILES * P], U8, align_bytes=64)
             codes_sb[u] = codes
             scales_sb[u] = scales
-            for g in range(GROUPS):
+            for groups in (slice(0, 2), slice(2, 3)):
                 nc.vector.quantize_mx(
-                    out=codes[:, g, :].bitcast(FP8X4),
-                    scales=scales[:, g, :],
-                    in_=grouped_sb[u][:, g, :],
+                    out=codes[:, groups, :].rearrange("p g c -> p (g c)").bitcast(FP8X4),
+                    scales=scales[:, groups, :].rearrange("p g c -> p (g c)"),
+                    in_=grouped_sb[u][:, groups, :].rearrange("p g c -> p (g c)"),
                 )
 
         def project(u):

@@ -20,6 +20,7 @@ GROUPS = 3
 K_GROUP = P * PACK
 EMB = 128
 EMB_ALL = GROUPS * EMB
+PASS_BASES = 2
 TILES = 2
 UNITS = BATCH // (TILES * P)
 CLIP = 1.0
@@ -69,18 +70,18 @@ def tile_gep_pa_t_kernel(tc, target_grad, bases0, bases1, bases2, out_0, out_1):
         nc.vector.memset(column_sums[:], 0.0)
         weighted = mean_psum.tile([P, GROUPS, P], F32)
 
-        base_grouped = const.tile([P, GROUPS, EMB, PACK], BF16, align_bytes=64)
+        base_grouped = const.tile([P, GROUPS + 1, EMB, PACK], BF16, align_bytes=64)
+        nc.vector.memset(base_grouped[:, GROUPS], 0.0)
         nc.vector.tensor_copy(
-            out=base_grouped[:], in_=base_rows[:].rearrange("p g t c -> p g c t")
+            out=base_grouped[:, 0:GROUPS], in_=base_rows[:].rearrange("p g t c -> p g c t")
         )
-        base_codes = const.tile([P, GROUPS, EMB], U32, align_bytes=64)
-        base_scales = const.tile([P, GROUPS, EMB], U8, align_bytes=64)
-        for g in range(GROUPS):
-            nc.vector.quantize_mx(
-                out=base_codes[:, g, :].bitcast(FP8X4),
-                scales=base_scales[:, g, :],
-                in_=base_grouped[:, g].rearrange("p c t -> p (c t)"),
-            )
+        base_codes = const.tile([P, (GROUPS + 1) * EMB], U32, align_bytes=64)
+        base_scales = const.tile([P, (GROUPS + 1) * EMB], U8, align_bytes=64)
+        nc.vector.quantize_mx(
+            out=base_codes[:].bitcast(FP8X4),
+            scales=base_scales[:],
+            in_=base_grouped[:].rearrange("p g c t -> p (g c t)"),
+        )
 
         grouped_sb = {}
         codes_sb = {}
@@ -131,15 +132,16 @@ def tile_gep_pa_t_kernel(tc, target_grad, bases0, bases1, bases2, out_0, out_1):
             accs = []
             for t in range(TILES):
                 rows = slice(t * P, (t + 1) * P)
-                acc = emb_psum.tile([P, EMB_ALL], F32)
+                acc = emb_psum.tile([P, (GROUPS + 1) * EMB], F32)
                 accs.append(acc)
                 for g in range(GROUPS):
+                    cols = slice(g * EMB, (g + PASS_BASES) * EMB)
                     nc.tensor.matmul_mx(
-                        out=acc[:, g * EMB : (g + 1) * EMB],
+                        out=acc[:, cols],
                         lhsT=codes_sb[u][:, g, rows].bitcast(FP8X4),
                         lhsT_scale=scales_sb[u][:, g, rows],
-                        rhs=base_codes[:, g, :].bitcast(FP8X4),
-                        rhs_scale=base_scales[:, g, :],
+                        rhs=base_codes[:, cols].bitcast(FP8X4),
+                        rhs_scale=base_scales[:, cols],
                         start=True,
                         stop=True,
                     )
@@ -147,12 +149,12 @@ def tile_gep_pa_t_kernel(tc, target_grad, bases0, bases1, bases2, out_0, out_1):
                 squares = stage.tile([P, EMB_ALL], F32)
                 nc.scalar.activation(
                     out=squares[:],
-                    in_=accs[t][:],
+                    in_=accs[t][:, 0:EMB_ALL],
                     func=ACT.Square,
                     accum_out=square_sum[:, t : t + 1],
                 )
             for t in range(TILES):
-                nc.scalar.copy(out=emb[:, t, :], in_=accs[t][:])
+                nc.scalar.copy(out=emb[:, t, :], in_=accs[t][:, 0:EMB_ALL])
             nc.sync.dma_start(out=emb_units[u], in_=emb[:].rearrange("p t j -> p (t j)"))
 
         def clip_factor(u):

from contextlib import ExitStack

import concourse.mybir as mybir
from concourse.masks import make_identity

F32 = mybir.dt.float32
BF16 = mybir.dt.bfloat16
U32 = mybir.dt.uint32
U8 = mybir.dt.uint8
FP8X4 = mybir.dt.float8_e4m3fn_x4
ACT = mybir.ActivationFunctionType
ALU = mybir.AluOpType
AXIS = mybir.AxisListType

P = 128
PACK = 4
HALVES = 2
BATCH = 4096
GROUPS = 3
K_GROUP = P * PACK
EMB = 128
EMB_ALL = GROUPS * EMB
PASS_BASES = 2
TILES = 2
UNITS = BATCH // (TILES * P)
CLIP = 1.0
SCALAR_BANKS = 3
OF_BANKS = 8

FLOPS = 2 * BATCH * GROUPS * K_GROUP * EMB


def tile_gep_pa_t_kernel(tc, target_grad, bases0, bases1, bases2, out_0, out_1):
    nc = tc.nc
    bases = [bases0, bases1, bases2]

    grad_pieces = target_grad.rearrange("(u p t) (g k) -> u g p t k", p=P, t=TILES, g=GROUPS)
    emb_units = out_0.rearrange("(u p t) j -> u p (t j)", p=P, t=TILES)

    with ExitStack() as ctx:
        ctx.enter_context(tc.manual_schedule())
        const = ctx.enter_context(tc.tile_pool(name="const", bufs=1))
        grads = ctx.enter_context(tc.tile_pool(name="grads", bufs=UNITS))
        stage = ctx.enter_context(tc.tile_pool(name="stage", bufs=3))
        embs = ctx.enter_context(tc.tile_pool(name="embs", bufs=UNITS))
        small = ctx.enter_context(tc.tile_pool(name="small", bufs=6))
        flipped_psum = ctx.enter_context(tc.psum_pool(name="flipped_psum", bufs=4))
        emb_psum = ctx.enter_context(tc.psum_pool(name="emb_psum", bufs=3))
        mean_psum = ctx.enter_context(tc.psum_pool(name="mean_psum", bufs=1))

        grad_sb = []
        for u in range(UNITS):
            grad = grads.tile([P, GROUPS, TILES, K_GROUP], BF16)
            for g in range(GROUPS):
                nc.sync.dma_start(out=grad[:, g], in_=grad_pieces[u, g])
            grad_sb.append(grad)

        base_rows = const.tile([P, GROUPS, PACK, EMB], BF16)
        for g in range(GROUPS):
            nc.scalar.dma_start(
                out=base_rows[:, g].rearrange("p (h e) c -> p h (e c)", h=HALVES),
                in_=bases[g].rearrange("(h p e) c -> p h (e c)", h=HALVES, p=P),
            )

        identity = const.tile([P, P], F32)
        make_identity(nc, identity[:])
        minus_half = const.tile([P, TILES], F32)
        nc.gpsimd.memset(minus_half[:], -0.5)
        column_sums = const.tile([P, P], F32)
        nc.vector.memset(column_sums[:], 0.0)
        weighted = mean_psum.tile([P, GROUPS, P], F32)

        base_grouped = const.tile([P, GROUPS + 1, EMB, PACK], BF16, align_bytes=64)
        nc.vector.memset(base_grouped[:, GROUPS], 0.0)
        nc.vector.tensor_copy(
            out=base_grouped[:, 0:GROUPS], in_=base_rows[:].rearrange("p g t c -> p g c t")
        )
        base_codes = const.tile([P, (GROUPS + 1) * EMB], U32, align_bytes=64)
        base_scales = const.tile([P, (GROUPS + 1) * EMB], U8, align_bytes=64)
        nc.vector.quantize_mx(
            out=base_codes[:].bitcast(FP8X4),
            scales=base_scales[:],
            in_=base_grouped[:].rearrange("p g c t -> p (g c t)"),
        )

        grouped_sb = {}
        codes_sb = {}
        scales_sb = {}
        emb_sb = {}
        square_sum_sb = {}
        factor_sb = {}
        scaled_sb = {}

        def flip_and_regroup(u):
            grouped = stage.tile([P, GROUPS, TILES * P * PACK], BF16, align_bytes=64)
            grouped_sb[u] = grouped
            for g in range(GROUPS):
                flipped = flipped_psum.tile([P, TILES, HALVES, P], F32)
                for t in range(TILES):
                    words = grad_sb[u][:, g, t, :].bitcast(F32)
                    for h in range(HALVES):
                        nc.tensor.transpose(
                            flipped[:, t, h, :], words[:, h * P : (h + 1) * P], identity[:]
                        )
                bank = u * GROUPS + g
                to_scalar = (bank * SCALAR_BANKS) % OF_BANKS < SCALAR_BANKS
                copy = nc.scalar.copy if to_scalar else nc.vector.tensor_copy
                copy(
                    out=grouped[:, g, :]
                    .bitcast(F32)
                    .rearrange("p (t b h) -> p t b h", t=TILES, h=HALVES),
                    in_=flipped[:].rearrange("p t h b -> p t b h"),
                )

        def quantise(u):
            codes = stage.tile([P, GROUPS, TILES * P], U32, align_bytes=64)
            scales = stage.tile([P, GROUPS, TILES * P], U8, align_bytes=64)
            codes_sb[u] = codes
            scales_sb[u] = scales
            for groups in (slice(0, 2), slice(2, 3)):
                nc.vector.quantize_mx(
                    out=codes[:, groups, :].rearrange("p g c -> p (g c)").bitcast(FP8X4),
                    scales=scales[:, groups, :].rearrange("p g c -> p (g c)"),
                    in_=grouped_sb[u][:, groups, :].rearrange("p g c -> p (g c)"),
                )

        def project(u):
            emb = embs.tile([P, TILES, EMB_ALL], F32)
            emb_sb[u] = emb
            square_sum = small.tile([P, TILES], F32)
            square_sum_sb[u] = square_sum
            accs = []
            for t in range(TILES):
                rows = slice(t * P, (t + 1) * P)
                acc = emb_psum.tile([P, (GROUPS + 1) * EMB], F32)
                accs.append(acc)
                for g in range(GROUPS):
                    cols = slice(g * EMB, (g + PASS_BASES) * EMB)
                    nc.tensor.matmul_mx(
                        out=acc[:, cols],
                        lhsT=codes_sb[u][:, g, rows].bitcast(FP8X4),
                        lhsT_scale=scales_sb[u][:, g, rows],
                        rhs=base_codes[:, cols].bitcast(FP8X4),
                        rhs_scale=base_scales[:, cols],
                        start=True,
                        stop=True,
                    )
            for t in range(TILES):
                squares = stage.tile([P, EMB_ALL], F32)
                nc.scalar.activation(
                    out=squares[:],
                    in_=accs[t][:, 0:EMB_ALL],
                    func=ACT.Square,
                    accum_out=square_sum[:, t : t + 1],
                )
            for t in range(TILES):
                nc.scalar.copy(out=emb[:, t, :], in_=accs[t][:, 0:EMB_ALL])
            nc.sync.dma_start(out=emb_units[u], in_=emb[:].rearrange("p t j -> p (t j)"))

        def clip_factor(u):
            floored = small.tile([P, TILES], F32)
            nc.gpsimd.tensor_scalar_max(floored[:], square_sum_sb[u][:], CLIP * CLIP)
            factor = small.tile([P, TILES], F32)
            factor_sb[u] = factor
            nc.gpsimd.tensor_tensor(out=factor[:], in0=floored[:], in1=minus_half[:], op=ALU.pow)

        def weigh(u):
            scaled = stage.tile([P, TILES, EMB_ALL], F32)
            scaled_sb[u] = scaled
            for t in range(TILES):
                nc.vector.tensor_scalar_mul(
                    scaled[:, t, :], emb_sb[u][:, t, :], factor_sb[u][:, t : t + 1]
                )

        def add_up(u):
            for t in range(TILES):
                for g in range(GROUPS):
                    nc.tensor.matmul(
                        out=weighted[:, g, :],
                        lhsT=scaled_sb[u][:, t, g * EMB : (g + 1) * EMB],
                        rhs=identity[:],
                        is_transpose=True,
                        start=(u == 0 and t == 0 and g == 0),
                        stop=(u == UNITS - 1 and t == TILES - 1 and g == GROUPS - 1),
                    )

        for step in range(UNITS + 3):
            if 0 <= step - 1 < UNITS:
                quantise(step - 1)
            if step < UNITS:
                flip_and_regroup(step)
            if 0 <= step - 3 < UNITS:
                add_up(step - 3)
            if 0 <= step - 1 < UNITS:
                project(step - 1)
                clip_factor(step - 1)
            if 0 <= step - 2 < UNITS:
                weigh(step - 2)

        nc.vector.tensor_reduce(
            out=column_sums[:, 0:GROUPS], in_=weighted[:], axis=AXIS.X, op=ALU.add
        )
        sums_flipped = flipped_psum.tile([P, TILES, HALVES, P], F32, tag="flipped")
        nc.tensor.transpose(sums_flipped[:, 0, 0, :], column_sums[:], identity[:])
        avg = const.tile([P, EMB], F32)
        nc.scalar.activation(
            out=avg[:], in_=sums_flipped[:, 0, 0, :], func=ACT.Copy, scale=CLIP / BATCH
        )
        nc.sync.dma_start(
            out=out_1.rearrange("(g j) -> g j", g=GROUPS), in_=avg[0:GROUPS, :]
        )
